import numpy as np
import ml_dtypes

BF16 = ml_dtypes.bfloat16


def bf(x):
    return np.asarray(x, np.float32).astype(BF16)


def f32(x):
    return np.asarray(x, np.float32)


def f64(x):
    return np.asarray(x).astype(np.float64)


def striped(idx):
    return np.tile(idx.reshape(-1, 16).T, (8, 1))


C, S, Q, D, H, N = 1024, 1024, 4, 512, 512, 2048
EPS = 1e-5
ALPHA = 1.6732632423543772848170429916717
SCALE = 1.0507009873554804934193349852946


def selu(v):
    return SCALE * (np.maximum(v, 0.0) + ALPHA * (np.exp(np.minimum(v, 0.0)) - 1.0))


def batchnorm(u, gamma, beta):
    m = u.mean(axis=1, keepdims=True)
    v = np.square(u - m).mean(axis=1, keepdims=True)
    return (u - m) / np.sqrt(v + EPS) * gamma + beta


def setup_inputs():
    x = f32(np.random.standard_normal((C, S)))
    w1 = bf(np.random.uniform(-1.0, 1.0, (Q * D, H)) / np.sqrt(D))
    gamma1 = f32(1.0 + 0.1 * np.random.standard_normal((Q * H, 1)))
    beta1 = f32(0.1 * np.random.standard_normal((Q * H, 1)))
    w2 = bf(np.random.uniform(-1.0, 1.0, (Q * H, H)) / np.sqrt(H))
    gamma2 = f32(1.0 + 0.1 * np.random.standard_normal((Q * H, 1)))
    beta2 = f32(0.1 * np.random.standard_normal((Q * H, 1)))
    idx = np.concatenate([np.random.permutation(S)[:D] for _ in range(Q)])
    return {"x": x, "w1": w1, "gamma1": gamma1, "beta1": beta1, "w2": w2, "gamma2": gamma2, "beta2": beta2, "offs": striped(idx)}


def reference(x, w1, gamma1, beta1, w2, gamma2, beta2, offs):
    idx = offs[:16].T.reshape(-1)
    p = f64(x)[:, idx].reshape(C, Q, D).transpose(1, 0, 2)
    u = np.matmul(p, f64(w1).reshape(Q, D, H))
    a = selu(batchnorm(u, f64(gamma1).reshape(Q, 1, H), f64(beta1).reshape(Q, 1, H)))
    t = np.matmul(a, f64(w2).reshape(Q, H, H))
    r = selu(batchnorm(t, f64(gamma2).reshape(Q, 1, H), f64(beta2).reshape(Q, 1, H)))
    return r.transpose(1, 0, 2).reshape(C, Q * H)

@@ -1,0 +1,187 @@
+import concourse.mybir as mybir
+from concourse.masks import make_identity
+
+F32, BF16, U16 = mybir.dt.float32, mybir.dt.bfloat16, mybir.dt.uint16
+ACT = mybir.ActivationFunctionType
+ALU = mybir.AluOpType
+
+P = 128
+C, S, Q, D, H = 1024, 1024, 4, 512, 512
+BANK = 512
+RECORD_BLOCKS = C // P
+RECORD_HALVES = C // BANK
+BLOCKS_PER_HALF = BANK // P
+CHUNKS = D // P
+OFFSET_COLUMNS = D // 16
+
+EPS = 1e-5
+ALPHA = 1.6732632423543772
+SCALE = 1.0507009873554805
+SA = SCALE * ALPHA
+LN_SA = 0.5642333055432538
+
+FLOPS = 2 * C * Q * (D * H + H * H)
+
+
+def tile_customnetwork_b_kernel(tc, x, w1, gamma1, beta1, w2, gamma2, beta2, offs, out):
+    nc = tc.nc
+    with (
+        tc.tile_pool(name="held", bufs=1) as held,
+        tc.tile_pool(name="picked", bufs=3) as picked_pool,
+        tc.tile_pool(name="operands", bufs=2) as operand_pool,
+        tc.tile_pool(name="work", bufs=3) as work,
+        tc.tile_pool(name="small", bufs=6) as small,
+        tc.psum_pool(name="products", bufs=5) as product_banks,
+        tc.psum_pool(name="flips", bufs=3) as flip_banks,
+    ):
+        offsets = held.tile([P, Q * OFFSET_COLUMNS], U16, name="offsets")
+        nc.sync.dma_start(offsets[:], offs)
+
+        x_blocks = [held.tile([P, S], F32, name=f"x{b}") for b in range(RECORD_BLOCKS)]
+        w1_nodes = [held.tile([P, CHUNKS, H], BF16, name=f"w1_{q}") for q in range(Q)]
+        w2_nodes = [held.tile([P, CHUNKS, H], BF16, name=f"w2_{q}") for q in range(Q)]
+        w1_view = w1.rearrange("(q k p) i -> q p k i", q=Q, p=P)
+        w2_view = w2.rearrange("(q k p) i -> q p k i", q=Q, p=P)
+        loads = [(x_blocks[b], x[b * P : (b + 1) * P, :]) for b in range(BLOCKS_PER_HALF)]
+        loads.append((w1_nodes[0], w1_view[0]))
+        loads.extend((x_blocks[b], x[b * P : (b + 1) * P, :]) for b in range(BLOCKS_PER_HALF, RECORD_BLOCKS))
+        for q in range(Q):
+            if q + 1 < Q:
+                loads.append((w1_nodes[q + 1], w1_view[q + 1]))
+            loads.append((w2_nodes[q], w2_view[q]))
+        for n, (tile, source) in enumerate(loads):
+            queue = nc.sync if n % 2 == 0 else nc.scalar
+            queue.dma_start(tile[:], source)
+
+        identity = held.tile([P, P], F32, name="identity")
+        make_identity(nc, identity[:])
+        minus_half = held.tile([P, 1], F32, name="minus_half")
+        nc.vector.memset(minus_half[:], -0.5)
+        exp2_bias = held.tile([P, 1], F32, name="exp2_bias")
+        nc.vector.memset(exp2_bias[:], ALPHA + LN_SA)
+
+        def load_vector(vector, name):
+            tile = held.tile([P, Q * CHUNKS], F32, name=name)
+            nc.gpsimd.dma_start(tile[:], vector.rearrange("(g p) o -> p (g o)", p=P))
+            return tile
+
+        g1, b1 = load_vector(gamma1, "g1"), load_vector(beta1, "b1")
+        g2, b2 = load_vector(gamma2, "g2"), load_vector(beta2, "b2")
+
+        gains1 = held.tile([P, 4, Q * CHUNKS], F32, name="gains1")
+        for n, factor in enumerate((1.0, SCALE, -1.0, -SCALE)):
+            nc.vector.tensor_scalar(gains1[:, n, :], g1[:], factor, None, op0=ALU.mult)
+        shifts1 = held.tile([P, 2, Q * CHUNKS], F32, name="shifts1")
+        nc.vector.tensor_scalar(shifts1[:, 0, :], b1[:], LN_SA, None, op0=ALU.add)
+        nc.vector.tensor_scalar(shifts1[:, 1, :], b1[:], SCALE, None, op0=ALU.mult)
+        gains2 = held.tile([P, 2, Q * CHUNKS], F32, name="gains2")
+        for n, factor in enumerate((SCALE, -SCALE)):
+            nc.vector.tensor_scalar(gains2[:, n, :], g2[:], factor, None, op0=ALU.mult)
+        shifts2 = held.tile([P, 1, Q * CHUNKS], F32, name="shifts2")
+        nc.vector.tensor_scalar(shifts2[:, 0, :], b2[:], SCALE, -SA, op0=ALU.mult, op1=ALU.add)
+
+        out_view = out.rearrange("(b p) n -> p b n", p=P)
+
+        def pick_block(q, b, picked_t):
+            picked = picked_pool.tile([P, D], F32, name="picked")
+            node_list = offsets[:, q * OFFSET_COLUMNS : (q + 1) * OFFSET_COLUMNS]
+            nc.scalar.activation(picked[:], x_blocks[b][:].indirect(node_list), ACT.Copy)
+            flipped = flip_banks.tile([P, BANK], F32, name="flipped", tag="flip")
+            for k in range(CHUNKS):
+                nc.tensor.transpose(flipped[:, k * P : (k + 1) * P], picked[:, k * P : (k + 1) * P], identity[:])
+            nc.vector.tensor_copy(
+                picked_t[:, :, b * P : (b + 1) * P], flipped[:].rearrange("p (k c) -> p k c", k=CHUNKS)
+            )
+
+        def product(weights, m, moving):
+            banks = []
+            for h in range(RECORD_HALVES):
+                bank = product_banks.tile([P, BANK], F32, name="bank", tag="product")
+                for k in range(CHUNKS):
+                    nc.tensor.matmul(
+                        bank[:],
+                        weights[:, k, m * P : (m + 1) * P],
+                        moving[:, k, h * BANK : (h + 1) * BANK],
+                        start=(k == 0),
+                        stop=(k == CHUNKS - 1),
+                    )
+                banks.append(bank)
+            return banks
+
+        def batch_norm(banks, gains, shifts, g):
+            n_forms = shifts.shape[1]
+            stats = small.tile([P, RECORD_HALVES * 6], F32, name="stats")
+            for h in range(RECORD_HALVES):
+                nc.vector.bn_stats(stats[:, h * 6 : (h + 1) * 6], banks[h][:])
+            mean_var = small.tile([P, 2], F32, name="mean_var")
+            nc.vector.bn_aggr(mean_var[:], stats[:])
+            var_eps = small.tile([P, 1], F32, name="var_eps")
+            nc.gpsimd.tensor_scalar(var_eps[:], mean_var[:, 1:2], EPS, None, op0=ALU.add)
+            rstd = small.tile([P, 1], F32, name="rstd")
+            nc.gpsimd.tensor_tensor(rstd[:], var_eps[:], minus_half[:], op=ALU.pow)
+            scale = small.tile([P, 2 * n_forms], F32, name="scale")
+            nc.gpsimd.tensor_scalar(scale[:], gains[:, :, g], rstd[:, 0:1], None, op0=ALU.mult)
+            shift = small.tile([P, n_forms], F32, name="shift")
+            nc.vector.scalar_tensor_tensor(
+                shift[:], scale[:, n_forms:], mean_var[:, 0:1], shifts[:, :, g], op0=ALU.mult, op1=ALU.add
+            )
+            return scale, shift
+
+        def layer1_chunk(q, m, picked_t, hidden_t):
+            banks = product(w1_nodes[q], m, picked_t)
+            scale, shift = batch_norm(banks, gains1, shifts1, q * CHUNKS + m)
+            grown = work.tile([P, C], F32, name="grown")
+            positive = work.tile([P, C], BF16, name="positive")
+            for h in range(RECORD_HALVES):
+                half = slice(h * BANK, (h + 1) * BANK)
+                nc.scalar.activation(grown[:, half], banks[h][:], ACT.Exp, bias=shift[:, 0:1], scale=scale[:, 0:1])
+                nc.scalar.activation(positive[:, half], banks[h][:], ACT.Relu, bias=shift[:, 1:2], scale=scale[:, 1:2])
+            negative = work.tile([P, C], BF16, name="negative")
+            nc.vector.tensor_scalar(negative[:], grown[:], -SA, 0.0, op0=ALU.add, op1=ALU.min)
+            nc.gpsimd.tensor_tensor(hidden_t[:, m, :], positive[:], negative[:], op=ALU.add)
+
+        def layer2_chunk(q, m, hidden_t):
+            banks = product(w2_nodes[q], m, hidden_t)
+            scale, shift = batch_norm(banks, gains2, shifts2, q * CHUNKS + m)
+            lowered = work.tile([P, C], F32, name="lowered")
+            for h in range(RECORD_HALVES):
+                nc.vector.tensor_scalar(
+                    lowered[:, h * BANK : (h + 1) * BANK], banks[h][:], scale[:, 0:1], shift[:, 0:1],
+                    op0=ALU.mult, op1=ALU.add,
+                )
+            for h in range(RECORD_HALVES):
+                flipped = flip_banks.tile([P, BANK], F32, name="flipped_out", tag="flip")
+                for j in range(BLOCKS_PER_HALF):
+                    b = h * BLOCKS_PER_HALF + j
+                    nc.tensor.transpose(flipped[:, j * P : (j + 1) * P], lowered[:, b * P : (b + 1) * P], identity[:])
+                grown = work.tile([P, BANK], F32, name="grown_out")
+                nc.scalar.activation(grown[:], flipped[:], ACT.Exp, bias=exp2_bias[:, 0:1], scale=1.0 / SCALE)
+                capped = work.tile([P, BANK], F32, name="capped")
+                nc.gpsimd.tensor_scalar(capped[:], grown[:], SA, 0.0, op0=ALU.min, op1=ALU.max)
+                result = work.tile([P, BANK], F32, name="result")
+                nc.vector.scalar_tensor_tensor(result[:], flipped[:], -SA, capped[:], op0=ALU.max, op1=ALU.add)
+                first = h * BLOCKS_PER_HALF
+                column = q * H + m * P
+                nc.sync.dma_start(
+                    out_view[:, first : first + BLOCKS_PER_HALF, column : column + P],
+                    result[:].rearrange("p (b k) -> p b k", b=BLOCKS_PER_HALF),
+                )
+
+        picked_ts, hidden_ts = {}, {}
+        picked_ts[0] = operand_pool.tile([P, CHUNKS, C], BF16, name="picked_t")
+        for b in range(RECORD_BLOCKS):
+            pick_block(0, b, picked_ts[0])
+        blocks_per_step = RECORD_BLOCKS // CHUNKS
+        for t in range(Q + 1):
+            if t + 1 < Q:
+                picked_ts[t + 1] = operand_pool.tile([P, CHUNKS, C], BF16, name="picked_t")
+            if t < Q:
+                hidden_ts[t] = operand_pool.tile([P, CHUNKS, C], BF16, name="hidden_t")
+            for m in range(CHUNKS):
+                if t >= 1:
+                    layer2_chunk(t - 1, m, hidden_ts[t - 1])
+                if t < Q:
+                    layer1_chunk(t, m, picked_ts[t], hidden_ts[t])
+                if t + 1 < Q:
+                    for b in range(m * blocks_per_step, (m + 1) * blocks_per_step):
+                        pick_block(t + 1, b, picked_ts[t + 1])

@@ -29,10 +29,10 @@ def tile_customnetwork_b_kernel(tc, x, w1, gamma1, beta1, w2, gamma2, beta2, off
         tc.tile_pool(name="held", bufs=1) as held,
         tc.tile_pool(name="picked", bufs=3) as picked_pool,
         tc.tile_pool(name="operands", bufs=2) as operand_pool,
-        tc.tile_pool(name="work", bufs=3) as work,
+        tc.tile_pool(name="work", bufs=4) as work,
         tc.tile_pool(name="small", bufs=6) as small,
-        tc.psum_pool(name="products", bufs=5) as product_banks,
-        tc.psum_pool(name="flips", bufs=3) as flip_banks,
+        tc.psum_pool(name="products", bufs=6) as product_banks,
+        tc.psum_pool(name="flips", bufs=2) as flip_banks,
     ):
         offsets = held.tile([P, Q * OFFSET_COLUMNS], U16, name="offsets")
         nc.sync.dma_start(offsets[:], offs)
@@ -49,36 +49,39 @@ def tile_customnetwork_b_kernel(tc, x, w1, gamma1, beta1, w2, gamma2, beta2, off
             if q + 1 < Q:
                 loads.append((w1_nodes[q + 1], w1_view[q + 1]))
             loads.append((w2_nodes[q], w2_view[q]))
-        for n, (tile, source) in enumerate(loads):
-            queue = nc.sync if n % 2 == 0 else nc.scalar
-            queue.dma_start(tile[:], source)
+        for tile, source in loads:
+            nc.sync.dma_start(tile[:], source)
 
         identity = held.tile([P, P], F32, name="identity")
         make_identity(nc, identity[:])
         minus_half = held.tile([P, 1], F32, name="minus_half")
         nc.vector.memset(minus_half[:], -0.5)
-        exp2_bias = held.tile([P, 1], F32, name="exp2_bias")
-        nc.vector.memset(exp2_bias[:], ALPHA + LN_SA)
 
-        def load_vector(vector, name):
-            tile = held.tile([P, Q * CHUNKS], F32, name=name)
-            nc.gpsimd.dma_start(tile[:], vector.rearrange("(g p) o -> p (g o)", p=P))
-            return tile
+        n_chunks = Q * CHUNKS
+        vector_rows = held.tile([4 * n_chunks, P], F32, name="vector_rows")
+        for v, vector in enumerate((gamma1, beta1, gamma2, beta2)):
+            nc.scalar.dma_start(
+                vector_rows[v * n_chunks : (v + 1) * n_chunks, :], vector.rearrange("(g p) o -> g (p o)", p=P)
+            )
+        vectors_flipped = flip_banks.tile([P, BANK], F32, name="vectors_flipped", tag="flip")
+        nc.tensor.transpose(
+            vectors_flipped[:, 0 : 4 * n_chunks], vector_rows[:], identity[0 : 4 * n_chunks, 0 : 4 * n_chunks]
+        )
+        vectors = held.tile([P, 4, n_chunks], F32, name="vectors")
+        nc.vector.tensor_copy(vectors[:], vectors_flipped[:, 0 : 4 * n_chunks].rearrange("p (v g) -> p v g", v=4))
+        g1, b1, g2, b2 = (vectors[:, v, :] for v in range(4))
 
-        g1, b1 = load_vector(gamma1, "g1"), load_vector(beta1, "b1")
-        g2, b2 = load_vector(gamma2, "g2"), load_vector(beta2, "b2")
+        def selu_forms(gamma, beta, layer):
+            gains = held.tile([P, 4, n_chunks], F32, name=f"gains{layer}")
+            for n, factor in enumerate((1.0, SCALE, -1.0, -SCALE)):
+                nc.vector.tensor_scalar(gains[:, n, :], gamma, factor, None, op0=ALU.mult)
+            shifts = held.tile([P, 2, n_chunks], F32, name=f"shifts{layer}")
+            nc.vector.tensor_scalar(shifts[:, 0, :], beta, LN_SA, None, op0=ALU.add)
+            nc.vector.tensor_scalar(shifts[:, 1, :], beta, SCALE, None, op0=ALU.mult)
+            return gains, shifts
 
-        gains1 = held.tile([P, 4, Q * CHUNKS], F32, name="gains1")
-        for n, factor in enumerate((1.0, SCALE, -1.0, -SCALE)):
-            nc.vector.tensor_scalar(gains1[:, n, :], g1[:], factor, None, op0=ALU.mult)
-        shifts1 = held.tile([P, 2, Q * CHUNKS], F32, name="shifts1")
-        nc.vector.tensor_scalar(shifts1[:, 0, :], b1[:], LN_SA, None, op0=ALU.add)
-        nc.vector.tensor_scalar(shifts1[:, 1, :], b1[:], SCALE, None, op0=ALU.mult)
-        gains2 = held.tile([P, 2, Q * CHUNKS], F32, name="gains2")
-        for n, factor in enumerate((SCALE, -SCALE)):
-            nc.vector.tensor_scalar(gains2[:, n, :], g2[:], factor, None, op0=ALU.mult)
-        shifts2 = held.tile([P, 1, Q * CHUNKS], F32, name="shifts2")
-        nc.vector.tensor_scalar(shifts2[:, 0, :], b2[:], SCALE, -SA, op0=ALU.mult, op1=ALU.add)
+        gains1, shifts1 = selu_forms(g1, b1, 1)
+        gains2, shifts2 = selu_forms(g2, b2, 2)
 
         out_view = out.rearrange("(b p) n -> p b n", p=P)
 
@@ -109,7 +112,6 @@ def tile_customnetwork_b_kernel(tc, x, w1, gamma1, beta1, w2, gamma2, beta2, off
             return banks
 
         def batch_norm(banks, gains, shifts, g):
-            n_forms = shifts.shape[1]
             stats = small.tile([P, RECORD_HALVES * 6], F32, name="stats")
             for h in range(RECORD_HALVES):
                 nc.vector.bn_stats(stats[:, h * 6 : (h + 1) * 6], banks[h][:])
@@ -119,69 +121,91 @@ def tile_customnetwork_b_kernel(tc, x, w1, gamma1, beta1, w2, gamma2, beta2, off
             nc.gpsimd.tensor_scalar(var_eps[:], mean_var[:, 1:2], EPS, None, op0=ALU.add)
             rstd = small.tile([P, 1], F32, name="rstd")
             nc.gpsimd.tensor_tensor(rstd[:], var_eps[:], minus_half[:], op=ALU.pow)
-            scale = small.tile([P, 2 * n_forms], F32, name="scale")
+            scale = small.tile([P, 4], F32, name="scale")
             nc.gpsimd.tensor_scalar(scale[:], gains[:, :, g], rstd[:, 0:1], None, op0=ALU.mult)
-            shift = small.tile([P, n_forms], F32, name="shift")
+            shift = small.tile([P, 2], F32, name="shift")
             nc.vector.scalar_tensor_tensor(
-                shift[:], scale[:, n_forms:], mean_var[:, 0:1], shifts[:, :, g], op0=ALU.mult, op1=ALU.add
+                shift[:], scale[:, 2:4], mean_var[:, 0:1], shifts[:, :, g], op0=ALU.mult, op1=ALU.add
             )
             return scale, shift
 
-        def layer1_chunk(q, m, picked_t, hidden_t):
-            banks = product(w1_nodes[q], m, picked_t)
-            scale, shift = batch_norm(banks, gains1, shifts1, q * CHUNKS + m)
-            grown = work.tile([P, C], F32, name="grown")
-            positive = work.tile([P, C], BF16, name="positive")
+        def selu(banks, scale, shift, activated):
             for h in range(RECORD_HALVES):
-                half = slice(h * BANK, (h + 1) * BANK)
-                nc.scalar.activation(grown[:, half], banks[h][:], ACT.Exp, bias=shift[:, 0:1], scale=scale[:, 0:1])
-                nc.scalar.activation(positive[:, half], banks[h][:], ACT.Relu, bias=shift[:, 1:2], scale=scale[:, 1:2])
-            negative = work.tile([P, C], BF16, name="negative")
-            nc.vector.tensor_scalar(negative[:], grown[:], -SA, 0.0, op0=ALU.add, op1=ALU.min)
-            nc.gpsimd.tensor_tensor(hidden_t[:, m, :], positive[:], negative[:], op=ALU.add)
-
-        def layer2_chunk(q, m, hidden_t):
-            banks = product(w2_nodes[q], m, hidden_t)
-            scale, shift = batch_norm(banks, gains2, shifts2, q * CHUNKS + m)
-            lowered = work.tile([P, C], F32, name="lowered")
-            for h in range(RECORD_HALVES):
-                nc.vector.tensor_scalar(
-                    lowered[:, h * BANK : (h + 1) * BANK], banks[h][:], scale[:, 0:1], shift[:, 0:1],
-                    op0=ALU.mult, op1=ALU.add,
+                grown = work.tile([P, BANK], F32, name="grown")
+                nc.scalar.activation(grown[:], banks[h][:], ACT.Exp, bias=shift[:, 0:1], scale=scale[:, 0:1])
+                positive = work.tile([P, BANK], F32, name="positive")
+                nc.scalar.activation(positive[:], banks[h][:], ACT.Relu, bias=shift[:, 1:2], scale=scale[:, 1:2])
+                nc.vector.scalar_tensor_tensor(
+                    activated[:, h * BANK : (h + 1) * BANK], grown[:], -SA, positive[:], op0=ALU.add, op1=ALU.min
                 )
+
+        def deliver(q, m, settled):
             for h in range(RECORD_HALVES):
                 flipped = flip_banks.tile([P, BANK], F32, name="flipped_out", tag="flip")
                 for j in range(BLOCKS_PER_HALF):
                     b = h * BLOCKS_PER_HALF + j
-                    nc.tensor.transpose(flipped[:, j * P : (j + 1) * P], lowered[:, b * P : (b + 1) * P], identity[:])
-                grown = work.tile([P, BANK], F32, name="grown_out")
-                nc.scalar.activation(grown[:], flipped[:], ACT.Exp, bias=exp2_bias[:, 0:1], scale=1.0 / SCALE)
-                capped = work.tile([P, BANK], F32, name="capped")
-                nc.gpsimd.tensor_scalar(capped[:], grown[:], SA, 0.0, op0=ALU.min, op1=ALU.max)
-                result = work.tile([P, BANK], F32, name="result")
-                nc.vector.scalar_tensor_tensor(result[:], flipped[:], -SA, capped[:], op0=ALU.max, op1=ALU.add)
+                    nc.tensor.transpose(flipped[:, j * P : (j + 1) * P], settled[:, b * P : (b + 1) * P], identity[:])
+                staged = work.tile([P, BANK], F32, name="staged")
+                nc.vector.tensor_copy(staged[:], flipped[:])
                 first = h * BLOCKS_PER_HALF
                 column = q * H + m * P
                 nc.sync.dma_start(
                     out_view[:, first : first + BLOCKS_PER_HALF, column : column + P],
-                    result[:].rearrange("p (b k) -> p b k", b=BLOCKS_PER_HALF),
+                    staged[:].rearrange("p (b k) -> p b k", b=BLOCKS_PER_HALF),
                 )
 
-        picked_ts, hidden_ts = {}, {}
-        picked_ts[0] = operand_pool.tile([P, CHUNKS, C], BF16, name="picked_t")
-        for b in range(RECORD_BLOCKS):
-            pick_block(0, b, picked_ts[0])
-        blocks_per_step = RECORD_BLOCKS // CHUNKS
+        slots = []
         for t in range(Q + 1):
-            if t + 1 < Q:
-                picked_ts[t + 1] = operand_pool.tile([P, CHUNKS, C], BF16, name="picked_t")
-            if t < Q:
-                hidden_ts[t] = operand_pool.tile([P, CHUNKS, C], BF16, name="hidden_t")
+            phase = []
             for m in range(CHUNKS):
-                if t >= 1:
-                    layer2_chunk(t - 1, m, hidden_ts[t - 1])
                 if t < Q:
-                    layer1_chunk(t, m, picked_ts[t], hidden_ts[t])
-                if t + 1 < Q:
-                    for b in range(m * blocks_per_step, (m + 1) * blocks_per_step):
-                        pick_block(t + 1, b, picked_ts[t + 1])
+                    phase.append((1, t, m))
+                if t >= 1:
+                    phase.append((2, t - 1, m))
+            picks_each = RECORD_BLOCKS // len(phase) if t + 1 < Q else 0
+            for n, chunk in enumerate(phase):
+                slots.append((chunk, [(t + 1, b) for b in range(n * picks_each, (n + 1) * picks_each)]))
+
+        picked_ts = {q: None for q in range(Q)}
+        hidden_ts = {q: None for q in range(Q)}
+        started = {}
+        settled_tiles = {}
+
+        def pick(q, b):
+            if picked_ts[q] is None:
+                picked_ts[q] = operand_pool.tile([P, CHUNKS, C], BF16, name="picked_t")
+            pick_block(q, b, picked_ts[q])
+
+        def start(chunk):
+            layer, q, m = chunk
+            if layer == 1:
+                banks = product(w1_nodes[q], m, picked_ts[q])
+                started[chunk] = (banks, batch_norm(banks, gains1, shifts1, q * CHUNKS + m))
+            else:
+                banks = product(w2_nodes[q], m, hidden_ts[q])
+                started[chunk] = (banks, batch_norm(banks, gains2, shifts2, q * CHUNKS + m))
+
+        def finish(chunk):
+            layer, q, m = chunk
+            banks, (scale, shift) = started[chunk]
+            if layer == 1:
+                if hidden_ts[q] is None:
+                    hidden_ts[q] = operand_pool.tile([P, CHUNKS, C], BF16, name="hidden_t")
+                selu(banks, scale, shift, hidden_ts[q][:, m, :])
+            else:
+                settled_tiles[chunk] = work.tile([P, C], F32, name="settled")
+                selu(banks, scale, shift, settled_tiles[chunk])
+
+        for b in range(RECORD_BLOCKS):
+            pick(0, b)
+        for s in range(len(slots) + 2):
+            if s < len(slots):
+                chunk, picks = slots[s]
+                for q, b in picks:
+                    pick(q, b)
+                start(chunk)
+            if 1 <= s <= len(slots):
+                finish(slots[s - 1][0])
+            if s >= 2 and slots[s - 2][0][0] == 2:
+                layer, q, m = slots[s - 2][0]
+                deliver(q, m, settled_tiles[slots[s - 2][0]])

@@ -27,10 +27,10 @@ def tile_customnetwork_b_kernel(tc, x, w1, gamma1, beta1, w2, gamma2, beta2, off
     nc = tc.nc
     with (
         tc.tile_pool(name="held", bufs=1) as held,
-        tc.tile_pool(name="picked", bufs=3) as picked_pool,
-        tc.tile_pool(name="operands", bufs=2) as operand_pool,
+        tc.tile_pool(name="picked", bufs=4) as picked_pool,
+        tc.tile_pool(name="operands", bufs=3) as operand_pool,
         tc.tile_pool(name="work", bufs=4) as work,
-        tc.tile_pool(name="small", bufs=6) as small,
+        tc.tile_pool(name="small", bufs=8) as small,
         tc.psum_pool(name="products", bufs=6) as product_banks,
         tc.psum_pool(name="flips", bufs=2) as flip_banks,
     ):
@@ -72,8 +72,8 @@ def tile_customnetwork_b_kernel(tc, x, w1, gamma1, beta1, w2, gamma2, beta2, off
         g1, b1, g2, b2 = (vectors[:, v, :] for v in range(4))
 
         def selu_forms(gamma, beta, layer):
-            gains = held.tile([P, 4, n_chunks], F32, name=f"gains{layer}")
-            for n, factor in enumerate((1.0, SCALE, -1.0, -SCALE)):
+            gains = held.tile([P, 2, n_chunks], F32, name=f"gains{layer}")
+            for n, factor in enumerate((1.0, SCALE)):
                 nc.vector.tensor_scalar(gains[:, n, :], gamma, factor, None, op0=ALU.mult)
             shifts = held.tile([P, 2, n_chunks], F32, name=f"shifts{layer}")
             nc.vector.tensor_scalar(shifts[:, 0, :], beta, LN_SA, None, op0=ALU.add)
@@ -85,19 +85,52 @@ def tile_customnetwork_b_kernel(tc, x, w1, gamma1, beta1, w2, gamma2, beta2, off
 
         out_view = out.rearrange("(b p) n -> p b n", p=P)
 
-        def pick_block(q, b, picked_t):
+        chunks = []
+        for t in range(Q + 1):
+            for m in range(CHUNKS):
+                if t < Q:
+                    chunks.append((1, t, m))
+                if t >= 1:
+                    chunks.append((2, t - 1, m))
+        lookups = {s: [] for s in range(-1, len(chunks))}
+        for q in range(1, Q):
+            begin = chunks.index((1, q - 1, 0)) - 1
+            end = chunks.index((1, q, 0)) - 1
+            for b in range(RECORD_BLOCKS):
+                lookups[begin + b * (end - begin) // RECORD_BLOCKS].append((q, b))
+
+        picked_ts = {q: None for q in range(Q)}
+        hidden_ts = {q: None for q in range(Q)}
+        picked_tiles, flipped_tiles = {}, {}
+        banks_of, mean_var_of, affine_of = {}, {}, {}
+        settled_of, flipped_out_of = {}, {}
+
+        def look_up(q, b):
             picked = picked_pool.tile([P, D], F32, name="picked")
             node_list = offsets[:, q * OFFSET_COLUMNS : (q + 1) * OFFSET_COLUMNS]
             nc.scalar.activation(picked[:], x_blocks[b][:].indirect(node_list), ACT.Copy)
+            picked_tiles[(q, b)] = picked
+
+        def flip_picked(q, b):
             flipped = flip_banks.tile([P, BANK], F32, name="flipped", tag="flip")
             for k in range(CHUNKS):
-                nc.tensor.transpose(flipped[:, k * P : (k + 1) * P], picked[:, k * P : (k + 1) * P], identity[:])
+                nc.tensor.transpose(
+                    flipped[:, k * P : (k + 1) * P], picked_tiles[(q, b)][:, k * P : (k + 1) * P], identity[:]
+                )
+            flipped_tiles[(q, b)] = flipped
+
+        def keep_picked(q, b):
+            if picked_ts[q] is None:
+                picked_ts[q] = operand_pool.tile([P, CHUNKS, C], BF16, name="picked_t")
             nc.vector.tensor_copy(
-                picked_t[:, :, b * P : (b + 1) * P], flipped[:].rearrange("p (k c) -> p k c", k=CHUNKS)
+                picked_ts[q][:, :, b * P : (b + 1) * P],
+                flipped_tiles[(q, b)][:].rearrange("p (k c) -> p k c", k=CHUNKS),
             )
 
-        def product(weights, m, moving):
-            banks = []
+        def multiply(chunk):
+            layer, q, m = chunk
+            weights, moving = (w1_nodes[q], picked_ts[q]) if layer == 1 else (w2_nodes[q], hidden_ts[q])
+            banks_of[chunk] = []
             for h in range(RECORD_HALVES):
                 bank = product_banks.tile([P, BANK], F32, name="bank", tag="product")
                 for k in range(CHUNKS):
@@ -108,45 +141,71 @@ def tile_customnetwork_b_kernel(tc, x, w1, gamma1, beta1, w2, gamma2, beta2, off
                         start=(k == 0),
                         stop=(k == CHUNKS - 1),
                     )
-                banks.append(bank)
-            return banks
+                banks_of[chunk].append(bank)
 
-        def batch_norm(banks, gains, shifts, g):
+        def measure(chunk):
             stats = small.tile([P, RECORD_HALVES * 6], F32, name="stats")
             for h in range(RECORD_HALVES):
-                nc.vector.bn_stats(stats[:, h * 6 : (h + 1) * 6], banks[h][:])
+                nc.vector.bn_stats(stats[:, h * 6 : (h + 1) * 6], banks_of[chunk][h][:])
+                if h == 0:
+                    nc.vector.tensor_scalar(stats[:, 2:3], stats[:, 2:3], C * EPS, None, op0=ALU.add)
             mean_var = small.tile([P, 2], F32, name="mean_var")
             nc.vector.bn_aggr(mean_var[:], stats[:])
-            var_eps = small.tile([P, 1], F32, name="var_eps")
-            nc.gpsimd.tensor_scalar(var_eps[:], mean_var[:, 1:2], EPS, None, op0=ALU.add)
+            mean_var_of[chunk] = mean_var
+
+        def scale_and_shift(chunk):
+            layer, q, m = chunk
+            gains, shifts = (gains1, shifts1) if layer == 1 else (gains2, shifts2)
+            g = q * CHUNKS + m
+            mean_var = mean_var_of[chunk]
             rstd = small.tile([P, 1], F32, name="rstd")
-            nc.gpsimd.tensor_tensor(rstd[:], var_eps[:], minus_half[:], op=ALU.pow)
-            scale = small.tile([P, 4], F32, name="scale")
-            nc.gpsimd.tensor_scalar(scale[:], gains[:, :, g], rstd[:, 0:1], None, op0=ALU.mult)
+            nc.gpsimd.tensor_tensor(rstd[:], mean_var[:, 1:2], minus_half[:], op=ALU.pow)
+            lowering = small.tile([P, 2], F32, name="lowering")
+            nc.vector.tensor_scalar(lowering[:], gains[:, :, g], mean_var[:, 0:1], -1.0, op0=ALU.mult, op1=ALU.mult)
+            scale = small.tile([P, 2], F32, name="scale")
+            nc.vector.tensor_scalar(scale[:], gains[:, :, g], rstd[:, 0:1], None, op0=ALU.mult)
             shift = small.tile([P, 2], F32, name="shift")
             nc.vector.scalar_tensor_tensor(
-                shift[:], scale[:, 2:4], mean_var[:, 0:1], shifts[:, :, g], op0=ALU.mult, op1=ALU.add
+                shift[:], lowering[:], rstd[:, 0:1], shifts[:, :, g], op0=ALU.mult, op1=ALU.add
             )
-            return scale, shift
+            affine_of[chunk] = (scale, shift)
 
-        def selu(banks, scale, shift, activated):
+        def activate(chunk):
+            layer, q, m = chunk
+            scale, shift = affine_of[chunk]
+            if layer == 1:
+                if hidden_ts[q] is None:
+                    hidden_ts[q] = operand_pool.tile([P, CHUNKS, C], BF16, name="hidden_t")
+                activated = hidden_ts[q][:, m, :]
+            else:
+                settled_of[chunk] = work.tile([P, C], F32, name="settled")
+                activated = settled_of[chunk]
             for h in range(RECORD_HALVES):
+                bank = banks_of[chunk][h]
                 grown = work.tile([P, BANK], F32, name="grown")
-                nc.scalar.activation(grown[:], banks[h][:], ACT.Exp, bias=shift[:, 0:1], scale=scale[:, 0:1])
+                nc.scalar.activation(grown[:], bank[:], ACT.Exp, bias=shift[:, 0:1], scale=scale[:, 0:1])
                 positive = work.tile([P, BANK], F32, name="positive")
-                nc.scalar.activation(positive[:], banks[h][:], ACT.Relu, bias=shift[:, 1:2], scale=scale[:, 1:2])
+                nc.scalar.activation(positive[:], bank[:], ACT.Relu, bias=shift[:, 1:2], scale=scale[:, 1:2])
                 nc.vector.scalar_tensor_tensor(
                     activated[:, h * BANK : (h + 1) * BANK], grown[:], -SA, positive[:], op0=ALU.add, op1=ALU.min
                 )
 
-        def deliver(q, m, settled):
+        def flip_settled(chunk):
+            flipped_out_of[chunk] = []
             for h in range(RECORD_HALVES):
                 flipped = flip_banks.tile([P, BANK], F32, name="flipped_out", tag="flip")
                 for j in range(BLOCKS_PER_HALF):
                     b = h * BLOCKS_PER_HALF + j
-                    nc.tensor.transpose(flipped[:, j * P : (j + 1) * P], settled[:, b * P : (b + 1) * P], identity[:])
+                    nc.tensor.transpose(
+                        flipped[:, j * P : (j + 1) * P], settled_of[chunk][:, b * P : (b + 1) * P], identity[:]
+                    )
+                flipped_out_of[chunk].append(flipped)
+
+        def store(chunk):
+            layer, q, m = chunk
+            for h in range(RECORD_HALVES):
                 staged = work.tile([P, BANK], F32, name="staged")
-                nc.vector.tensor_copy(staged[:], flipped[:])
+                nc.vector.tensor_copy(staged[:], flipped_out_of[chunk][h][:])
                 first = h * BLOCKS_PER_HALF
                 column = q * H + m * P
                 nc.sync.dma_start(
@@ -154,58 +213,30 @@ def tile_customnetwork_b_kernel(tc, x, w1, gamma1, beta1, w2, gamma2, beta2, off
                     staged[:].rearrange("p (b k) -> p b k", b=BLOCKS_PER_HALF),
                 )
 
-        slots = []
-        for t in range(Q + 1):
-            phase = []
-            for m in range(CHUNKS):
-                if t < Q:
-                    phase.append((1, t, m))
-                if t >= 1:
-                    phase.append((2, t - 1, m))
-            picks_each = RECORD_BLOCKS // len(phase) if t + 1 < Q else 0
-            for n, chunk in enumerate(phase):
-                slots.append((chunk, [(t + 1, b) for b in range(n * picks_each, (n + 1) * picks_each)]))
-
-        picked_ts = {q: None for q in range(Q)}
-        hidden_ts = {q: None for q in range(Q)}
-        started = {}
-        settled_tiles = {}
-
-        def pick(q, b):
-            if picked_ts[q] is None:
-                picked_ts[q] = operand_pool.tile([P, CHUNKS, C], BF16, name="picked_t")
-            pick_block(q, b, picked_ts[q])
-
-        def start(chunk):
-            layer, q, m = chunk
-            if layer == 1:
-                banks = product(w1_nodes[q], m, picked_ts[q])
-                started[chunk] = (banks, batch_norm(banks, gains1, shifts1, q * CHUNKS + m))
-            else:
-                banks = product(w2_nodes[q], m, hidden_ts[q])
-                started[chunk] = (banks, batch_norm(banks, gains2, shifts2, q * CHUNKS + m))
-
-        def finish(chunk):
-            layer, q, m = chunk
-            banks, (scale, shift) = started[chunk]
-            if layer == 1:
-                if hidden_ts[q] is None:
-                    hidden_ts[q] = operand_pool.tile([P, CHUNKS, C], BF16, name="hidden_t")
-                selu(banks, scale, shift, hidden_ts[q][:, m, :])
-            else:
-                settled_tiles[chunk] = work.tile([P, C], F32, name="settled")
-                selu(banks, scale, shift, settled_tiles[chunk])
+        def chunk_at(s):
+            return chunks[s] if 0 <= s < len(chunks) else None
 
         for b in range(RECORD_BLOCKS):
-            pick(0, b)
-        for s in range(len(slots) + 2):
-            if s < len(slots):
-                chunk, picks = slots[s]
-                for q, b in picks:
-                    pick(q, b)
-                start(chunk)
-            if 1 <= s <= len(slots):
-                finish(slots[s - 1][0])
-            if s >= 2 and slots[s - 2][0][0] == 2:
-                layer, q, m = slots[s - 2][0]
-                deliver(q, m, settled_tiles[slots[s - 2][0]])
+            look_up(0, b)
+            flip_picked(0, b)
+            keep_picked(0, b)
+        for s in range(-1, len(chunks) + 3):
+            begun, multiplied, activated_before = chunk_at(s), chunk_at(s - 1), chunk_at(s - 3)
+            if begun:
+                multiply(begun)
+            for q, b in lookups.get(s - 1, []):
+                flip_picked(q, b)
+            if activated_before and activated_before[0] == 2:
+                flip_settled(activated_before)
+            if begun:
+                measure(begun)
+            for q, b in lookups.get(s, []):
+                look_up(q, b)
+            for q, b in lookups.get(s - 1, []):
+                keep_picked(q, b)
+            if multiplied:
+                activate(multiplied)
+            if activated_before and activated_before[0] == 2:
+                store(activated_before)
+            if begun:
+                scale_and_shift(begun)

@@ -13,6 +13,7 @@ RECORD_HALVES = C // BANK
 BLOCKS_PER_HALF = BANK // P
 CHUNKS = D // P
 OFFSET_COLUMNS = D // 16
+CHUNKS_IN_PSUM = 3
 
 EPS = 1e-5
 ALPHA = 1.6732632423543772
@@ -31,7 +32,7 @@ def tile_customnetwork_b_kernel(tc, x, w1, gamma1, beta1, w2, gamma2, beta2, off
         tc.tile_pool(name="operands", bufs=3) as operand_pool,
         tc.tile_pool(name="work", bufs=4) as work,
         tc.tile_pool(name="small", bufs=8) as small,
-        tc.psum_pool(name="products", bufs=6) as product_banks,
+        tc.psum_pool(name="products", bufs=CHUNKS_IN_PSUM * RECORD_HALVES) as product_banks,
         tc.psum_pool(name="flips", bufs=2) as flip_banks,
     ):
         offsets = held.tile([P, Q * OFFSET_COLUMNS], U16, name="offsets")
@@ -72,16 +73,22 @@ def tile_customnetwork_b_kernel(tc, x, w1, gamma1, beta1, w2, gamma2, beta2, off
         g1, b1, g2, b2 = (vectors[:, v, :] for v in range(4))
 
         def selu_forms(gamma, beta, layer):
-            gains = held.tile([P, 2, n_chunks], F32, name=f"gains{layer}")
-            for n, factor in enumerate((1.0, SCALE)):
-                nc.vector.tensor_scalar(gains[:, n, :], gamma, factor, None, op0=ALU.mult)
-            shifts = held.tile([P, 2, n_chunks], F32, name=f"shifts{layer}")
-            nc.vector.tensor_scalar(shifts[:, 0, :], beta, LN_SA, None, op0=ALU.add)
-            nc.vector.tensor_scalar(shifts[:, 1, :], beta, SCALE, None, op0=ALU.mult)
-            return gains, shifts
+            factors = held.tile([P, n_chunks, 4], F32, name=f"factors{layer}")
+            nc.vector.tensor_copy(factors[:, :, 0], gamma)
+            nc.vector.tensor_scalar(factors[:, :, 1], gamma, SCALE, None, op0=ALU.mult)
+            addends = held.tile([P, n_chunks, 4], F32, name=f"addends{layer}")
+            nc.vector.memset(addends[:], 0.0)
+            nc.vector.tensor_scalar(addends[:, :, 2], beta, LN_SA, None, op0=ALU.add)
+            nc.vector.tensor_scalar(addends[:, :, 3], beta, SCALE, None, op0=ALU.mult)
+            return factors, addends
 
-        gains1, shifts1 = selu_forms(g1, b1, 1)
-        gains2, shifts2 = selu_forms(g2, b2, 2)
+        factors1, addends1 = selu_forms(g1, b1, 1)
+        factors2, addends2 = selu_forms(g2, b2, 2)
+
+        stats_ring = [held.tile([P, RECORD_HALVES * 6 + 3], F32, name=f"stats{n}") for n in range(CHUNKS_IN_PSUM)]
+        for stats in stats_ring:
+            nc.vector.memset(stats[:, RECORD_HALVES * 6 : RECORD_HALVES * 6 + 2], 0.0)
+            nc.vector.memset(stats[:, RECORD_HALVES * 6 + 2 : RECORD_HALVES * 6 + 3], C * EPS)
 
         out_view = out.rearrange("(b p) n -> p b n", p=P)
 
@@ -98,6 +105,7 @@ def tile_customnetwork_b_kernel(tc, x, w1, gamma1, beta1, w2, gamma2, beta2, off
             end = chunks.index((1, q, 0)) - 1
             for b in range(RECORD_BLOCKS):
                 lookups[begin + b * (end - begin) // RECORD_BLOCKS].append((q, b))
+        last_lookup_slot = max(s for s in lookups if lookups[s])
 
         picked_ts = {q: None for q in range(Q)}
         hidden_ts = {q: None for q in range(Q)}
@@ -144,31 +152,28 @@ def tile_customnetwork_b_kernel(tc, x, w1, gamma1, beta1, w2, gamma2, beta2, off
                 banks_of[chunk].append(bank)
 
         def measure(chunk):
-            stats = small.tile([P, RECORD_HALVES * 6], F32, name="stats")
+            stats = stats_ring[chunks.index(chunk) % CHUNKS_IN_PSUM]
             for h in range(RECORD_HALVES):
                 nc.vector.bn_stats(stats[:, h * 6 : (h + 1) * 6], banks_of[chunk][h][:])
-                if h == 0:
-                    nc.vector.tensor_scalar(stats[:, 2:3], stats[:, 2:3], C * EPS, None, op0=ALU.add)
             mean_var = small.tile([P, 2], F32, name="mean_var")
             nc.vector.bn_aggr(mean_var[:], stats[:])
             mean_var_of[chunk] = mean_var
 
         def scale_and_shift(chunk):
             layer, q, m = chunk
-            gains, shifts = (gains1, shifts1) if layer == 1 else (gains2, shifts2)
+            factors, addends = (factors1, addends1) if layer == 1 else (factors2, addends2)
             g = q * CHUNKS + m
             mean_var = mean_var_of[chunk]
             rstd = small.tile([P, 1], F32, name="rstd")
             nc.gpsimd.tensor_tensor(rstd[:], mean_var[:, 1:2], minus_half[:], op=ALU.pow)
-            lowering = small.tile([P, 2], F32, name="lowering")
-            nc.vector.tensor_scalar(lowering[:], gains[:, :, g], mean_var[:, 0:1], -1.0, op0=ALU.mult, op1=ALU.mult)
-            scale = small.tile([P, 2], F32, name="scale")
-            nc.vector.tensor_scalar(scale[:], gains[:, :, g], rstd[:, 0:1], None, op0=ALU.mult)
-            shift = small.tile([P, 2], F32, name="shift")
-            nc.vector.scalar_tensor_tensor(
-                shift[:], lowering[:], rstd[:, 0:1], shifts[:, :, g], op0=ALU.mult, op1=ALU.add
+            nc.vector.tensor_scalar(
+                factors[:, g, 2:4], factors[:, g, 0:2], mean_var[:, 0:1], -1.0, op0=ALU.mult, op1=ALU.mult
             )
-            affine_of[chunk] = (scale, shift)
+            affine = small.tile([P, 4], F32, name="affine")
+            nc.vector.scalar_tensor_tensor(
+                affine[:], factors[:, g, :], rstd[:, 0:1], addends[:, g, :], op0=ALU.mult, op1=ALU.add
+            )
+            affine_of[chunk] = (affine[:, 0:2], affine[:, 2:4])
 
         def activate(chunk):
             layer, q, m = chunk
@@ -201,11 +206,14 @@ def tile_customnetwork_b_kernel(tc, x, w1, gamma1, beta1, w2, gamma2, beta2, off
                     )
                 flipped_out_of[chunk].append(flipped)
 
-        def store(chunk):
+        def store(chunk, scalar_helps):
             layer, q, m = chunk
             for h in range(RECORD_HALVES):
                 staged = work.tile([P, BANK], F32, name="staged")
-                nc.vector.tensor_copy(staged[:], flipped_out_of[chunk][h][:])
+                if scalar_helps and h == 1:
+                    nc.scalar.copy(staged[:], flipped_out_of[chunk][h][:])
+                else:
+                    nc.vector.tensor_copy(staged[:], flipped_out_of[chunk][h][:])
                 first = h * BLOCKS_PER_HALF
                 column = q * H + m * P
                 nc.sync.dma_start(
@@ -237,6 +245,6 @@ def tile_customnetwork_b_kernel(tc, x, w1, gamma1, beta1, w2, gamma2, beta2, off
             if multiplied:
                 activate(multiplied)
             if activated_before and activated_before[0] == 2:
-                store(activated_before)
+                store(activated_before, scalar_helps=(s > last_lookup_slot))
             if begun:
                 scale_and_shift(begun)

@@ -28,13 +28,18 @@ def tile_customnetwork_b_kernel(tc, x, w1, gamma1, beta1, w2, gamma2, beta2, off
     nc = tc.nc
     with (
         tc.tile_pool(name="held", bufs=1) as held,
-        tc.tile_pool(name="picked", bufs=4) as picked_pool,
+        tc.tile_pool(name="picked", bufs=2) as picked_pool,
         tc.tile_pool(name="operands", bufs=3) as operand_pool,
         tc.tile_pool(name="work", bufs=4) as work,
         tc.tile_pool(name="small", bufs=8) as small,
         tc.psum_pool(name="products", bufs=CHUNKS_IN_PSUM * RECORD_HALVES) as product_banks,
         tc.psum_pool(name="flips", bufs=2) as flip_banks,
     ):
+        minus_half = held.tile([P, 1], F32, name="minus_half")
+        nc.vector.memset(minus_half[:], -0.5)
+        warmed = held.tile([P, 1], F32, name="warmed")
+        nc.scalar.activation(warmed[:], minus_half[:], ACT.Exp)
+
         offsets = held.tile([P, Q * OFFSET_COLUMNS], U16, name="offsets")
         nc.sync.dma_start(offsets[:], offs)
 
@@ -55,8 +60,6 @@ def tile_customnetwork_b_kernel(tc, x, w1, gamma1, beta1, w2, gamma2, beta2, off
 
         identity = held.tile([P, P], F32, name="identity")
         make_identity(nc, identity[:])
-        minus_half = held.tile([P, 1], F32, name="minus_half")
-        nc.vector.memset(minus_half[:], -0.5)
 
         n_chunks = Q * CHUNKS
         vector_rows = held.tile([4 * n_chunks, P], F32, name="vector_rows")
@@ -238,12 +241,12 @@ def tile_customnetwork_b_kernel(tc, x, w1, gamma1, beta1, w2, gamma2, beta2, off
                 flip_settled(activated_before)
             if begun:
                 measure(begun)
-            for q, b in lookups.get(s, []):
-                look_up(q, b)
             for q, b in lookups.get(s - 1, []):
                 keep_picked(q, b)
             if multiplied:
                 activate(multiplied)
+            for q, b in lookups.get(s, []):
+                look_up(q, b)
             if activated_before and activated_before[0] == 2:
                 store(activated_before, scalar_helps=(s > last_lookup_slot))
             if begun:

@@ -231,8 +231,8 @@ def tile_customnetwork_b_kernel(tc, x, w1, gamma1, beta1, w2, gamma2, beta2, off
             look_up(0, b)
             flip_picked(0, b)
             keep_picked(0, b)
-        for s in range(-1, len(chunks) + 3):
-            begun, multiplied, activated_before = chunk_at(s), chunk_at(s - 1), chunk_at(s - 3)
+        for s in range(-1, len(chunks) + 2):
+            begun, multiplied, activated_before = chunk_at(s), chunk_at(s - 1), chunk_at(s - 2)
             if begun:
                 multiply(begun)
             for q, b in lookups.get(s - 1, []):

@@ -235,18 +235,16 @@ def tile_customnetwork_b_kernel(tc, x, w1, gamma1, beta1, w2, gamma2, beta2, off
             begun, multiplied, activated_before = chunk_at(s), chunk_at(s - 1), chunk_at(s - 2)
             if begun:
                 multiply(begun)
-            for q, b in lookups.get(s - 1, []):
-                flip_picked(q, b)
             if activated_before and activated_before[0] == 2:
                 flip_settled(activated_before)
             if begun:
                 measure(begun)
-            for q, b in lookups.get(s - 1, []):
-                keep_picked(q, b)
             if multiplied:
                 activate(multiplied)
             for q, b in lookups.get(s, []):
                 look_up(q, b)
+                flip_picked(q, b)
+                keep_picked(q, b)
             if activated_before and activated_before[0] == 2:
                 store(activated_before, scalar_helps=(s > last_lookup_slot))
             if begun:

import concourse.mybir as mybir
from concourse.masks import make_identity

F32, BF16, U16 = mybir.dt.float32, mybir.dt.bfloat16, mybir.dt.uint16
ACT = mybir.ActivationFunctionType
ALU = mybir.AluOpType

P = 128
C, S, Q, D, H = 1024, 1024, 4, 512, 512
BANK = 512
RECORD_BLOCKS = C // P
RECORD_HALVES = C // BANK
BLOCKS_PER_HALF = BANK // P
CHUNKS = D // P
OFFSET_COLUMNS = D // 16
CHUNKS_IN_PSUM = 3

EPS = 1e-5
ALPHA = 1.6732632423543772
SCALE = 1.0507009873554805
SA = SCALE * ALPHA
LN_SA = 0.5642333055432538

FLOPS = 2 * C * Q * (D * H + H * H)


def tile_customnetwork_b_kernel(tc, x, w1, gamma1, beta1, w2, gamma2, beta2, offs, out):
    nc = tc.nc
    with (
        tc.tile_pool(name="held", bufs=1) as held,
        tc.tile_pool(name="picked", bufs=2) as picked_pool,
        tc.tile_pool(name="operands", bufs=3) as operand_pool,
        tc.tile_pool(name="work", bufs=4) as work,
        tc.tile_pool(name="small", bufs=8) as small,
        tc.psum_pool(name="products", bufs=CHUNKS_IN_PSUM * RECORD_HALVES) as product_banks,
        tc.psum_pool(name="flips", bufs=2) as flip_banks,
    ):
        minus_half = held.tile([P, 1], F32, name="minus_half")
        nc.vector.memset(minus_half[:], -0.5)
        warmed = held.tile([P, 1], F32, name="warmed")
        nc.scalar.activation(warmed[:], minus_half[:], ACT.Exp)

        offsets = held.tile([P, Q * OFFSET_COLUMNS], U16, name="offsets")
        nc.sync.dma_start(offsets[:], offs)

        x_blocks = [held.tile([P, S], F32, name=f"x{b}") for b in range(RECORD_BLOCKS)]
        w1_nodes = [held.tile([P, CHUNKS, H], BF16, name=f"w1_{q}") for q in range(Q)]
        w2_nodes = [held.tile([P, CHUNKS, H], BF16, name=f"w2_{q}") for q in range(Q)]
        w1_view = w1.rearrange("(q k p) i -> q p k i", q=Q, p=P)
        w2_view = w2.rearrange("(q k p) i -> q p k i", q=Q, p=P)
        loads = [(x_blocks[b], x[b * P : (b + 1) * P, :]) for b in range(BLOCKS_PER_HALF)]
        loads.append((w1_nodes[0], w1_view[0]))
        loads.extend((x_blocks[b], x[b * P : (b + 1) * P, :]) for b in range(BLOCKS_PER_HALF, RECORD_BLOCKS))
        for q in range(Q):
            if q + 1 < Q:
                loads.append((w1_nodes[q + 1], w1_view[q + 1]))
            loads.append((w2_nodes[q], w2_view[q]))
        for tile, source in loads:
            nc.sync.dma_start(tile[:], source)

        identity = held.tile([P, P], F32, name="identity")
        make_identity(nc, identity[:])

        n_chunks = Q * CHUNKS
        vector_rows = held.tile([4 * n_chunks, P], F32, name="vector_rows")
        for v, vector in enumerate((gamma1, beta1, gamma2, beta2)):
            nc.scalar.dma_start(
                vector_rows[v * n_chunks : (v + 1) * n_chunks, :], vector.rearrange("(g p) o -> g (p o)", p=P)
            )
        vectors_flipped = flip_banks.tile([P, BANK], F32, name="vectors_flipped", tag="flip")
        nc.tensor.transpose(
            vectors_flipped[:, 0 : 4 * n_chunks], vector_rows[:], identity[0 : 4 * n_chunks, 0 : 4 * n_chunks]
        )
        vectors = held.tile([P, 4, n_chunks], F32, name="vectors")
        nc.vector.tensor_copy(vectors[:], vectors_flipped[:, 0 : 4 * n_chunks].rearrange("p (v g) -> p v g", v=4))
        g1, b1, g2, b2 = (vectors[:, v, :] for v in range(4))

        def selu_forms(gamma, beta, layer):
            factors = held.tile([P, n_chunks, 4], F32, name=f"factors{layer}")
            nc.vector.tensor_copy(factors[:, :, 0], gamma)
            nc.vector.tensor_scalar(factors[:, :, 1], gamma, SCALE, None, op0=ALU.mult)
            addends = held.tile([P, n_chunks, 4], F32, name=f"addends{layer}")
            nc.vector.memset(addends[:], 0.0)
            nc.vector.tensor_scalar(addends[:, :, 2], beta, LN_SA, None, op0=ALU.add)
            nc.vector.tensor_scalar(addends[:, :, 3], beta, SCALE, None, op0=ALU.mult)
            return factors, addends

        factors1, addends1 = selu_forms(g1, b1, 1)
        factors2, addends2 = selu_forms(g2, b2, 2)

        stats_ring = [held.tile([P, RECORD_HALVES * 6 + 3], F32, name=f"stats{n}") for n in range(CHUNKS_IN_PSUM)]
        for stats in stats_ring:
            nc.vector.memset(stats[:, RECORD_HALVES * 6 : RECORD_HALVES * 6 + 2], 0.0)
            nc.vector.memset(stats[:, RECORD_HALVES * 6 + 2 : RECORD_HALVES * 6 + 3], C * EPS)

        out_view = out.rearrange("(b p) n -> p b n", p=P)

        chunks = []
        for t in range(Q + 1):
            for m in range(CHUNKS):
                if t < Q:
                    chunks.append((1, t, m))
                if t >= 1:
                    chunks.append((2, t - 1, m))
        lookups = {s: [] for s in range(-1, len(chunks))}
        for q in range(1, Q):
            begin = chunks.index((1, q - 1, 0)) - 1
            end = chunks.index((1, q, 0)) - 1
            for b in range(RECORD_BLOCKS):
                lookups[begin + b * (end - begin) // RECORD_BLOCKS].append((q, b))
        last_lookup_slot = max(s for s in lookups if lookups[s])

        picked_ts = {q: None for q in range(Q)}
        hidden_ts = {q: None for q in range(Q)}
        picked_tiles, flipped_tiles = {}, {}
        banks_of, mean_var_of, affine_of = {}, {}, {}
        settled_of, flipped_out_of = {}, {}

        def look_up(q, b):
            picked = picked_pool.tile([P, D], F32, name="picked")
            node_list = offsets[:, q * OFFSET_COLUMNS : (q + 1) * OFFSET_COLUMNS]
            nc.scalar.activation(picked[:], x_blocks[b][:].indirect(node_list), ACT.Copy)
            picked_tiles[(q, b)] = picked

        def flip_picked(q, b):
            flipped = flip_banks.tile([P, BANK], F32, name="flipped", tag="flip")
            for k in range(CHUNKS):
                nc.tensor.transpose(
                    flipped[:, k * P : (k + 1) * P], picked_tiles[(q, b)][:, k * P : (k + 1) * P], identity[:]
                )
            flipped_tiles[(q, b)] = flipped

        def keep_picked(q, b):
            if picked_ts[q] is None:
                picked_ts[q] = operand_pool.tile([P, CHUNKS, C], BF16, name="picked_t")
            nc.vector.tensor_copy(
                picked_ts[q][:, :, b * P : (b + 1) * P],
                flipped_tiles[(q, b)][:].rearrange("p (k c) -> p k c", k=CHUNKS),
            )

        def multiply(chunk):
            layer, q, m = chunk
            weights, moving = (w1_nodes[q], picked_ts[q]) if layer == 1 else (w2_nodes[q], hidden_ts[q])
            banks_of[chunk] = []
            for h in range(RECORD_HALVES):
                bank = product_banks.tile([P, BANK], F32, name="bank", tag="product")
                for k in range(CHUNKS):
                    nc.tensor.matmul(
                        bank[:],
                        weights[:, k, m * P : (m + 1) * P],
                        moving[:, k, h * BANK : (h + 1) * BANK],
                        start=(k == 0),
                        stop=(k == CHUNKS - 1),
                    )
                banks_of[chunk].append(bank)

        def measure(chunk):
            stats = stats_ring[chunks.index(chunk) % CHUNKS_IN_PSUM]
            for h in range(RECORD_HALVES):
                nc.vector.bn_stats(stats[:, h * 6 : (h + 1) * 6], banks_of[chunk][h][:])
            mean_var = small.tile([P, 2], F32, name="mean_var")
            nc.vector.bn_aggr(mean_var[:], stats[:])
            mean_var_of[chunk] = mean_var

        def scale_and_shift(chunk):
            layer, q, m = chunk
            factors, addends = (factors1, addends1) if layer == 1 else (factors2, addends2)
            g = q * CHUNKS + m
            mean_var = mean_var_of[chunk]
            rstd = small.tile([P, 1], F32, name="rstd")
            nc.gpsimd.tensor_tensor(rstd[:], mean_var[:, 1:2], minus_half[:], op=ALU.pow)
            nc.vector.tensor_scalar(
                factors[:, g, 2:4], factors[:, g, 0:2], mean_var[:, 0:1], -1.0, op0=ALU.mult, op1=ALU.mult
            )
            affine = small.tile([P, 4], F32, name="affine")
            nc.vector.scalar_tensor_tensor(
                affine[:], factors[:, g, :], rstd[:, 0:1], addends[:, g, :], op0=ALU.mult, op1=ALU.add
            )
            affine_of[chunk] = (affine[:, 0:2], affine[:, 2:4])

        def activate(chunk):
            layer, q, m = chunk
            scale, shift = affine_of[chunk]
            if layer == 1:
                if hidden_ts[q] is None:
                    hidden_ts[q] = operand_pool.tile([P, CHUNKS, C], BF16, name="hidden_t")
                activated = hidden_ts[q][:, m, :]
            else:
                settled_of[chunk] = work.tile([P, C], F32, name="settled")
                activated = settled_of[chunk]
            for h in range(RECORD_HALVES):
                bank = banks_of[chunk][h]
                grown = work.tile([P, BANK], F32, name="grown")
                nc.scalar.activation(grown[:], bank[:], ACT.Exp, bias=shift[:, 0:1], scale=scale[:, 0:1])
                positive = work.tile([P, BANK], F32, name="positive")
                nc.scalar.activation(positive[:], bank[:], ACT.Relu, bias=shift[:, 1:2], scale=scale[:, 1:2])
                nc.vector.scalar_tensor_tensor(
                    activated[:, h * BANK : (h + 1) * BANK], grown[:], -SA, positive[:], op0=ALU.add, op1=ALU.min
                )

        def flip_settled(chunk):
            flipped_out_of[chunk] = []
            for h in range(RECORD_HALVES):
                flipped = flip_banks.tile([P, BANK], F32, name="flipped_out", tag="flip")
                for j in range(BLOCKS_PER_HALF):
                    b = h * BLOCKS_PER_HALF + j
                    nc.tensor.transpose(
                        flipped[:, j * P : (j + 1) * P], settled_of[chunk][:, b * P : (b + 1) * P], identity[:]
                    )
                flipped_out_of[chunk].append(flipped)

        def store(chunk, scalar_helps):
            layer, q, m = chunk
            for h in range(RECORD_HALVES):
                staged = work.tile([P, BANK], F32, name="staged")
                if scalar_helps and h == 1:
                    nc.scalar.copy(staged[:], flipped_out_of[chunk][h][:])
                else:
                    nc.vector.tensor_copy(staged[:], flipped_out_of[chunk][h][:])
                first = h * BLOCKS_PER_HALF
                column = q * H + m * P
                nc.sync.dma_start(
                    out_view[:, first : first + BLOCKS_PER_HALF, column : column + P],
                    staged[:].rearrange("p (b k) -> p b k", b=BLOCKS_PER_HALF),
                )

        def chunk_at(s):
            return chunks[s] if 0 <= s < len(chunks) else None

        for b in range(RECORD_BLOCKS):
            look_up(0, b)
            flip_picked(0, b)
            keep_picked(0, b)
        for s in range(-1, len(chunks) + 2):
            begun, multiplied, activated_before = chunk_at(s), chunk_at(s - 1), chunk_at(s - 2)
            if begun:
                multiply(begun)
            if activated_before and activated_before[0] == 2:
                flip_settled(activated_before)
            if begun:
                measure(begun)
            if multiplied:
                activate(multiplied)
            for q, b in lookups.get(s, []):
                look_up(q, b)
                flip_picked(q, b)
                keep_picked(q, b)
            if activated_before and activated_before[0] == 2:
                store(activated_before, scalar_helps=(s > last_lookup_slot))
            if begun:
                scale_and_shift(begun)
